import numpy as np
import ml_dtypes


def mxq(x, axis, fmt="e4m3"):
    dtype, down = {"e4m3": (ml_dtypes.float8_e4m3fn, 7), "e5m2": (ml_dtypes.float8_e5m2, 14)}[fmt]
    v = np.moveaxis(np.asarray(x, np.float32).astype(ml_dtypes.bfloat16).astype(np.float64), axis, -1)
    blocks = v.reshape(v.shape[:-1] + (-1, 32))
    amax = np.abs(blocks).max(-1, keepdims=True)
    byte = np.maximum(np.where(amax > 0, np.frexp(amax)[1] - 1 + 127, 0) - down, 1)
    scale = np.exp2(byte - 127.0)
    codes = (blocks / scale).astype(np.float32).astype(dtype).astype(np.float64)
    return np.moveaxis((codes * scale).reshape(v.shape), -1, axis)


WIDE = False


def mx_kscale(k):
    if not WIDE:
        return np.ones(k)
    levels = np.array([18, -18])
    if k % 512:
        return np.exp2(np.random.permutation(np.resize(levels, k // 32))).repeat(32)
    a = np.empty((k // 512, 16))
    for p in range(k // 512):
        a[p, :8] = np.random.permutation(np.resize(levels, 8))
        for g in range(8):
            far = levels[np.abs(levels - a[p, g]) >= 10]
            a[p, g + 8] = far[np.random.randint(len(far))]
    return np.exp2(a.ravel()).repeat(32)


BF16 = ml_dtypes.bfloat16


def bf(x):
    return np.asarray(x, np.float32).astype(BF16)


def f64(x):
    return np.asarray(x).astype(np.float64)


B, D, U, L, G, P, NG = 2048, 256, 512, 3, 5, 3, 4
NB = G + P
C = (1 + L) * U


def silu(v):
    return v / (1.0 + np.exp(-v))


def knots():
    return -1.0 + (2.0 / G) * np.arange(-P, G + P + 1)


def bspline_basis(x, grid, k):
    xe = x[..., None]
    b = np.where((xe >= grid[:-1]) & (xe < grid[1:]), 1.0, 0.0)
    for p in range(1, k + 1):
        left = (xe - grid[:-(p + 1)]) / (grid[p:-1] - grid[:-(p + 1)]) * b[..., :-1]
        right = (grid[p + 1:] - xe) / (grid[p + 1:] - grid[1:-p]) * b[..., 1:]
        b = left + right
    return b


def kan_layers(x, kan_base_w, kan_spline_w):
    xf = f64(x)
    bases = bspline_basis(xf, knots(), P).reshape(B, D * NB)
    kan_out = silu(xf) @ f64(kan_base_w) + bases @ f64(kan_spline_w)
    return kan_out.transpose(1, 0, 2).reshape(B, L * U)


def setup_inputs():
    s = mx_kscale(B)
    s = (s / np.min(s))[:, None]
    u = mx_kscale(U)
    x = bf(np.random.standard_normal((B, D)))
    h0 = bf(np.random.standard_normal((B, U)) * 0.3)
    kan_base_w = bf(np.random.standard_normal((L, D, U)) / np.sqrt(D))
    kan_spline_w = bf(np.random.standard_normal((L, D * NB, U)) / np.sqrt(D))
    w0 = bf(np.random.standard_normal((C, U)) / np.sqrt(C))
    combine_b = bf(np.random.standard_normal(U) * 0.2)
    kan_concat = kan_layers(x, kan_base_w, kan_spline_w)
    g = bf(np.random.standard_normal((B, U)) * np.exp2(np.random.randint(-6, 1, (B, 1))) / s * u)
    return {
        "x": x,
        "lstm_out": bf(f64(h0) * s),
        "kan_base_w": kan_base_w,
        "kan_spline_w": kan_spline_w,
        "combine_w": bf(f64(w0) / u),
        "combine_b": combine_b,
        "kan_concat": np.asarray(kan_concat, np.float32),
        "grad_out": g,
    }


def reference(x, lstm_out, kan_base_w, kan_spline_w, combine_w, combine_b, kan_concat, grad_out):
    g = f64(grad_out)
    combined = np.concatenate([f64(lstm_out), f64(kan_concat)], axis=1)
    wl = f64(combine_w)[:U]
    d_lstm = mxq(g, 1, "e5m2") @ mxq(wl, 1, "e4m3").T
    d_w = mxq(combined, 0, "e4m3").T @ mxq(g, 0, "e5m2")
    return d_lstm, d_w

@@ -1,0 +1,192 @@
+from contextlib import ExitStack
+
+import concourse.mybir as mybir
+from concourse.masks import make_identity
+
+TOKENS, UNITS, KAN_COLS = 2048, 512, 1536
+FLOPS = 2 * TOKENS * UNITS * UNITS + 2 * TOKENS * (UNITS + KAN_COLS) * UNITS
+BYTES = TOKENS * KAN_COLS * 4 + 2 * TOKENS * UNITS * 2 + UNITS * UNITS * 2 + 2 * TOKENS * UNITS * 4
+
+F32 = mybir.dt.float32
+BF16 = mybir.dt.bfloat16
+U32 = mybir.dt.uint32
+U8 = mybir.dt.uint8
+E4M3 = mybir.dt.float8_e4m3fn_x4
+E5M2 = mybir.dt.float8_e5m2_x4
+
+P = 128
+PACK = 4
+K_PASS = P * PACK
+PASSES = TOKENS // K_PASS
+WIDTH = 512
+BLOCKS = WIDTH // P
+CHUNKS = (UNITS + KAN_COLS) // WIDTH
+SCALAR_COLS = 176
+RUN = 4
+
+
+def tile_tkancell_pa_v_kernel(
+    tc, x, lstm_out, kan_base_w, kan_spline_w, combine_w, combine_b, kan_concat, grad_out, out_0, out_1
+):
+    nc = tc.nc
+    with ExitStack() as ctx:
+        keep = ctx.enter_context(tc.tile_pool(name="keep", bufs=1))
+        wide = ctx.enter_context(tc.tile_pool(name="wide", bufs=18))
+        stage = ctx.enter_context(tc.tile_pool(name="stage", bufs=4))
+        psum = ctx.enter_context(tc.psum_pool(name="psum", bufs=8))
+        ctx.enter_context(tc.manual_schedule())
+
+        def load_pairs(name, src, half):
+            pair = keep.tile([P, 2, PACK * WIDTH], BF16, name="%s%d" % (name, half), align_bytes=64)
+            rows = src[2 * K_PASS * half : 2 * K_PASS * (half + 1), :]
+            nc.sync.dma_start(out=pair[:], in_=rows.rearrange("(g p j) w -> p g (j w)", g=2, j=PACK))
+            return [pair[:, g, :].rearrange("p (j w) -> p j w", j=PACK) for g in range(2)]
+
+        grad_rows = load_pairs("grad", grad_out, 0)
+        w_tile = keep.tile([P, PACK, WIDTH], BF16, name="w_rows", align_bytes=64)
+        nc.sync.dma_start(out=w_tile[:], in_=combine_w[0:UNITS, :].rearrange("(p j) w -> p j w", j=PACK))
+        grad_rows = grad_rows + load_pairs("grad", grad_out, 1)
+        combined_rows = [load_pairs("lstm", lstm_out, 0) + load_pairs("lstm", lstm_out, 1)]
+        for q in range(CHUNKS - 1):
+            rows_q = []
+            for g in range(PASSES):
+                kan_tile = wide.tile([P, PACK, WIDTH], F32, name="kan", tag="wide", align_bytes=64)
+                src = kan_concat[g * K_PASS : (g + 1) * K_PASS, q * WIDTH : (q + 1) * WIDTH]
+                nc.sync.dma_start(out=kan_tile[:], in_=src.rearrange("(p j) w -> p j w", j=PACK))
+                rows_q.append(kan_tile[:])
+            combined_rows.append(rows_q)
+
+        identity = keep.tile([P, P], F32, name="identity")
+        make_identity(nc, identity[:])
+
+        def new_grouped():
+            return stage.tile([P, WIDTH, PACK], BF16, name="grouped", align_bytes=64)
+
+        def new_bank():
+            return psum.tile([P, WIDTH], F32, name="bank")
+
+        def transpose_rows(rows, order):
+            grouped = new_grouped()
+            words = rows.bitcast(F32)
+            grouped_words = grouped[:].rearrange("p c t -> p (c t)").bitcast(F32)
+            banks = []
+            for h in range(2):
+                bank = new_bank()
+                for jj in range(2):
+                    for u in range(2):
+                        col = (2 * jj + u) * P
+                        nc.tensor.transpose(bank[:, col : col + P], words[:, 2 * h + jj, u : WIDTH // 2 : 2], identity[:])
+                banks.append(bank)
+            for h in range(2):
+                dst = grouped_words.rearrange("p (%s u) -> p j r u" % order, j=PACK, u=2)[:, 2 * h : 2 * h + 2]
+                src = banks[h][:].rearrange("p (j u r) -> p j r u", j=2, u=2)
+                if order == "r j":
+                    dst = dst.rearrange("p j r u -> p r j u")
+                    src = src.rearrange("p j r u -> p r j u")
+                nc.scalar.copy(out=dst, in_=src)
+            return grouped
+
+        def interleave_rows(rows, scalar_cols):
+            grouped = new_grouped()
+            dst = grouped[:].rearrange("p (c i) t -> p c t i", i=RUN)
+            src = rows.rearrange("p t (c i) -> p c t i", i=RUN)
+            cut = scalar_cols // RUN
+            if cut:
+                nc.scalar.copy(out=dst[:, :cut], in_=src[:, :cut])
+            nc.vector.tensor_copy(out=dst[:, cut:], in_=src[:, cut:])
+            return grouped
+
+        def quantize(grouped, fmt, pool, name):
+            codes = pool.tile([P, WIDTH], U32, name=name + "_codes", align_bytes=64)
+            scales = pool.tile([P, WIDTH], U8, name=name + "_scales", align_bytes=64)
+            nc.vector.quantize_mx(
+                out=codes[:].bitcast(fmt), scales=scales[:], in_=grouped[:].rearrange("p c t -> p (c t)")
+            )
+            return codes, scales, fmt
+
+        def multiply(banks, stationary, moving, start, stop):
+            for m in range(BLOCKS):
+                cols = slice(m * P, (m + 1) * P)
+                nc.tensor.matmul_mx(
+                    out=banks[m][:],
+                    lhsT=stationary[0][:, cols].bitcast(stationary[2]),
+                    lhsT_scale=stationary[1][:, cols],
+                    rhs=moving[0][:].bitcast(moving[2]),
+                    rhs_scale=moving[1][:],
+                    start=start,
+                    stop=stop,
+                )
+
+        units = [("w", 0, 0)]
+        for g in range(PASSES):
+            units.extend([("gf", 0, g), ("gt", 0, g)])
+        for q in range(CHUNKS):
+            units.extend([("c", q, g) for g in range(PASSES)])
+
+        grouped_of = {}
+        quantized = {}
+        banks_of = {}
+        pending = []
+
+        def prepare(unit):
+            kind, q, g = unit
+            if kind == "w":
+                grouped_of[unit] = transpose_rows(w_tile[:], "r j")
+            elif kind == "gf":
+                grouped_of[unit] = transpose_rows(grad_rows[g], "j r")
+            elif kind == "gt":
+                grouped_of[unit] = interleave_rows(grad_rows[g], 0)
+            else:
+                grouped_of[unit] = interleave_rows(combined_rows[q][g], SCALAR_COLS)
+
+        def quantize_unit(unit):
+            kind, q, g = unit
+            if kind == "w":
+                quantized[unit] = quantize(grouped_of[unit], E4M3, keep, "w")
+            elif kind == "gf":
+                quantized[unit] = quantize(grouped_of[unit], E5M2, stage, "lhs")
+            elif kind == "gt":
+                quantized[unit] = quantize(grouped_of[unit], E5M2, keep, "grad_tok%d" % g)
+            else:
+                quantized[unit] = quantize(grouped_of[unit], E4M3, stage, "lhs")
+
+        def finish(banks, dst):
+            result = wide.tile([P, BLOCKS, WIDTH], F32, name="result", tag="wide", align_bytes=64)
+            for m in range(BLOCKS):
+                pending.append((banks[m], result, m, dst))
+
+        def multiply_unit(unit):
+            kind, q, g = unit
+            if kind == "gf":
+                banks = [new_bank() for m in range(BLOCKS)]
+                multiply(banks, quantized[unit], quantized[("w", 0, 0)], True, True)
+                finish(banks, out_0[g * K_PASS : (g + 1) * K_PASS, :].rearrange("(p j) w -> p j w", j=PACK))
+            elif kind == "c":
+                if g == 0:
+                    banks_of[q] = [new_bank() for m in range(BLOCKS)]
+                multiply(banks_of[q], quantized[unit], quantized[("gt", 0, g)], g == 0, g == PASSES - 1)
+                if g == PASSES - 1:
+                    finish(banks_of[q], out_1[q * WIDTH : (q + 1) * WIDTH, :].rearrange("(m p) w -> p m w", p=P))
+
+        def evacuate(count, share_with_vector):
+            batch, rest = pending[:count], pending[count:]
+            pending.clear()
+            pending.extend(rest)
+            for n, (bank, result, m, dst) in enumerate(batch):
+                if share_with_vector and n % 2 == 1:
+                    nc.vector.tensor_copy(out=result[:, m, :], in_=bank[:])
+                else:
+                    nc.scalar.copy(out=result[:, m, :], in_=bank[:])
+                if m == BLOCKS - 1:
+                    nc.sync.dma_start(out=dst, in_=result[:])
+
+        first_c = 1 + 2 * PASSES
+        for step in range(-1, len(units) + 1):
+            if step + 1 < len(units):
+                prepare(units[step + 1])
+            if 0 <= step < len(units):
+                quantize_unit(units[step])
+            evacuate(BLOCKS if step <= first_c else 1, False)
+            if 0 <= step - 1:
+                multiply_unit(units[step - 1])
+        evacuate(len(pending), True)

@@ -21,7 +21,7 @@ PASSES = TOKENS // K_PASS
 WIDTH = 512
 BLOCKS = WIDTH // P
 CHUNKS = (UNITS + KAN_COLS) // WIDTH
-SCALAR_COLS = 176
+SCALAR_COLS = 224
 RUN = 4
 
 
@@ -31,30 +31,32 @@ def tile_tkancell_pa_v_kernel(
     nc = tc.nc
     with ExitStack() as ctx:
         keep = ctx.enter_context(tc.tile_pool(name="keep", bufs=1))
-        wide = ctx.enter_context(tc.tile_pool(name="wide", bufs=18))
+        wide = ctx.enter_context(tc.tile_pool(name="wide", bufs=2))
         stage = ctx.enter_context(tc.tile_pool(name="stage", bufs=4))
         psum = ctx.enter_context(tc.psum_pool(name="psum", bufs=8))
         ctx.enter_context(tc.manual_schedule())
 
-        def load_pairs(name, src, half):
-            pair = keep.tile([P, 2, PACK * WIDTH], BF16, name="%s%d" % (name, half), align_bytes=64)
-            rows = src[2 * K_PASS * half : 2 * K_PASS * (half + 1), :]
-            nc.sync.dma_start(out=pair[:], in_=rows.rearrange("(g p j) w -> p g (j w)", g=2, j=PACK))
-            return [pair[:, g, :].rearrange("p (j w) -> p j w", j=PACK) for g in range(2)]
+        def load_one(name, src, g):
+            rows = keep.tile([P, PACK, src.shape[1]], src.dtype, name="%s%d" % (name, g), align_bytes=64)
+            nc.sync.dma_start(
+                out=rows[:], in_=src[g * K_PASS : (g + 1) * K_PASS, :].rearrange("(p j) w -> p j w", j=PACK)
+            )
+            return rows[:]
 
-        grad_rows = load_pairs("grad", grad_out, 0)
-        w_tile = keep.tile([P, PACK, WIDTH], BF16, name="w_rows", align_bytes=64)
-        nc.sync.dma_start(out=w_tile[:], in_=combine_w[0:UNITS, :].rearrange("(p j) w -> p j w", j=PACK))
-        grad_rows = grad_rows + load_pairs("grad", grad_out, 1)
-        combined_rows = [load_pairs("lstm", lstm_out, 0) + load_pairs("lstm", lstm_out, 1)]
-        for q in range(CHUNKS - 1):
-            rows_q = []
-            for g in range(PASSES):
-                kan_tile = wide.tile([P, PACK, WIDTH], F32, name="kan", tag="wide", align_bytes=64)
-                src = kan_concat[g * K_PASS : (g + 1) * K_PASS, q * WIDTH : (q + 1) * WIDTH]
-                nc.sync.dma_start(out=kan_tile[:], in_=src.rearrange("(p j) w -> p j w", j=PACK))
-                rows_q.append(kan_tile[:])
-            combined_rows.append(rows_q)
+        def load_many(pool, name, src, first, count):
+            many = pool.tile([P, count, PACK * WIDTH], BF16, name=name, tag=name, align_bytes=64)
+            rows = src[first * K_PASS : (first + count) * K_PASS, :]
+            nc.sync.dma_start(out=many[:], in_=rows.rearrange("(g p j) w -> p g (j w)", g=count, j=PACK))
+            return [many[:, n, :].rearrange("p (j w) -> p j w", j=PACK) for n in range(count)]
+
+        grad_rows = [load_one("grad", grad_out, 0)]
+        w_rows = load_one("w", combine_w, 0)
+        grad_rows = grad_rows + load_many(keep, "grad_rest", grad_out, 1, PASSES - 1)
+        lstm_rows = load_many(wide, "wide", lstm_out, 0, PASSES)
+        kan_rows = [load_one("kan", kan_concat, g) for g in range(PASSES)]
+
+        def combined_rows(q, g):
+            return lstm_rows[g] if q == 0 else kan_rows[g][:, :, (q - 1) * WIDTH : q * WIDTH]
 
         identity = keep.tile([P, P], F32, name="identity")
         make_identity(nc, identity[:])
@@ -86,13 +88,20 @@ def tile_tkancell_pa_v_kernel(
                 nc.scalar.copy(out=dst, in_=src)
             return grouped
 
-        def interleave_rows(rows, scalar_cols):
+        def interleave_grad(rows):
             grouped = new_grouped()
-            dst = grouped[:].rearrange("p (c i) t -> p c t i", i=RUN)
-            src = rows.rearrange("p t (c i) -> p c t i", i=RUN)
-            cut = scalar_cols // RUN
-            if cut:
-                nc.scalar.copy(out=dst[:, :cut], in_=src[:, :cut])
+            nc.vector.tensor_copy(
+                out=grouped[:].rearrange("p (c i) t -> p c t i", i=RUN),
+                in_=rows.rearrange("p t (c i) -> p c t i", i=RUN),
+            )
+            return grouped
+
+        def interleave_combined(rows):
+            grouped = new_grouped()
+            dst = grouped[:].rearrange("p (e c i) t -> p c t i e", e=2, i=RUN // 2)
+            src = rows.rearrange("p t (c i e) -> p c t i e", e=2, i=RUN // 2)
+            cut = SCALAR_COLS // RUN
+            nc.scalar.copy(out=dst[:, :cut], in_=src[:, :cut])
             nc.vector.tensor_copy(out=dst[:, cut:], in_=src[:, cut:])
             return grouped
 
@@ -104,40 +113,32 @@ def tile_tkancell_pa_v_kernel(
             )
             return codes, scales, fmt
 
-        def multiply(banks, stationary, moving, start, stop):
-            for m in range(BLOCKS):
-                cols = slice(m * P, (m + 1) * P)
-                nc.tensor.matmul_mx(
-                    out=banks[m][:],
-                    lhsT=stationary[0][:, cols].bitcast(stationary[2]),
-                    lhsT_scale=stationary[1][:, cols],
-                    rhs=moving[0][:].bitcast(moving[2]),
-                    rhs_scale=moving[1][:],
-                    start=start,
-                    stop=stop,
-                )
-
-        units = [("w", 0, 0)]
-        for g in range(PASSES):
-            units.extend([("gf", 0, g), ("gt", 0, g)])
-        for q in range(CHUNKS):
-            units.extend([("c", q, g) for g in range(PASSES)])
+        def multiply(bank, m, stationary, moving, start, stop):
+            cols = slice(m * P, (m + 1) * P)
+            nc.tensor.matmul_mx(
+                out=bank[:],
+                lhsT=stationary[0][:, cols].bitcast(stationary[2]),
+                lhsT_scale=stationary[1][:, cols],
+                rhs=moving[0][:].bitcast(moving[2]),
+                rhs_scale=moving[1][:],
+                start=start,
+                stop=stop,
+            )
 
         grouped_of = {}
         quantized = {}
         banks_of = {}
-        pending = []
 
         def prepare(unit):
             kind, q, g = unit
             if kind == "w":
-                grouped_of[unit] = transpose_rows(w_tile[:], "r j")
+                grouped_of[unit] = transpose_rows(w_rows, "r j")
             elif kind == "gf":
                 grouped_of[unit] = transpose_rows(grad_rows[g], "j r")
             elif kind == "gt":
-                grouped_of[unit] = interleave_rows(grad_rows[g], 0)
+                grouped_of[unit] = interleave_grad(grad_rows[g])
             else:
-                grouped_of[unit] = interleave_rows(combined_rows[q][g], SCALAR_COLS)
+                grouped_of[unit] = interleave_combined(combined_rows(q, g))
 
         def quantize_unit(unit):
             kind, q, g = unit
@@ -147,46 +148,95 @@ def tile_tkancell_pa_v_kernel(
                 quantized[unit] = quantize(grouped_of[unit], E5M2, stage, "lhs")
             elif kind == "gt":
                 quantized[unit] = quantize(grouped_of[unit], E5M2, keep, "grad_tok%d" % g)
+            elif q == CHUNKS - 1:
+                quantized[unit] = quantize(grouped_of[unit], E4M3, keep, "late%d" % g)
             else:
                 quantized[unit] = quantize(grouped_of[unit], E4M3, stage, "lhs")
 
-        def finish(banks, dst):
-            result = wide.tile([P, BLOCKS, WIDTH], F32, name="result", tag="wide", align_bytes=64)
-            for m in range(BLOCKS):
-                pending.append((banks[m], result, m, dst))
+        def evacuate(banks, result, vector_blocks):
+            for n in range(BLOCKS):
+                if n in vector_blocks:
+                    nc.vector.tensor_copy(out=result[:, n, :], in_=banks[n][:])
+                else:
+                    nc.scalar.copy(out=result[:, n, :], in_=banks[n][:])
+
+        def multiply_chunk(q, passes):
+            if passes[0] == 0:
+                banks_of[q] = [new_bank() for m in range(BLOCKS)]
+            for n in range(BLOCKS):
+                for g in passes:
+                    stationary, moving = quantized[("c", q, g)], quantized[("gt", 0, g)]
+                    block = 2 * (n % 2) + n // 2
+                    multiply(banks_of[q][n], block, stationary, moving, g == 0, g == PASSES - 1)
+
+        result_0 = keep.tile([P, PASSES, BLOCKS, WIDTH], F32, name="result_0")
+        results_1 = {}
+
+        def evacuate_chunk(q):
+            if q % 2 == 0:
+                results_1[q // 2] = wide.tile([P, 2, BLOCKS, WIDTH], F32, name="result_1", tag="wide", align_bytes=64)
+            evacuate(banks_of[q], results_1[q // 2][:, q % 2], (1, 3))
+
+        def store_halves(first, count):
+            src = results_1[first // 4][:].rearrange("p q (h e) w -> p (q h) (e w)", e=2)
+            rows = out_1[first * 2 * P : (first + count) * 2 * P, :]
+            nc.sync.dma_start(
+                out=rows.rearrange("(h p e) w -> p h (e w)", p=P, e=2),
+                in_=src[:, first % 4 : first % 4 + count, :],
+            )
 
         def multiply_unit(unit):
             kind, q, g = unit
             if kind == "gf":
-                banks = [new_bank() for m in range(BLOCKS)]
-                multiply(banks, quantized[unit], quantized[("w", 0, 0)], True, True)
-                finish(banks, out_0[g * K_PASS : (g + 1) * K_PASS, :].rearrange("(p j) w -> p j w", j=PACK))
-            elif kind == "c":
-                if g == 0:
-                    banks_of[q] = [new_bank() for m in range(BLOCKS)]
-                multiply(banks_of[q], quantized[unit], quantized[("gt", 0, g)], g == 0, g == PASSES - 1)
+                banks_of[unit] = [new_bank() for m in range(BLOCKS)]
+                for m in range(BLOCKS):
+                    multiply(banks_of[unit][m], m, quantized[unit], quantized[("w", 0, 0)], True, True)
+            elif kind == "c" and q < CHUNKS - 1:
+                multiply_chunk(q, [g])
+
+        def evacuate_unit(unit):
+            kind, q, g = unit
+            if kind == "gf":
+                evacuate(banks_of[unit], result_0[:, g], (3,))
                 if g == PASSES - 1:
-                    finish(banks_of[q], out_1[q * WIDTH : (q + 1) * WIDTH, :].rearrange("(m p) w -> p m w", p=P))
+                    nc.sync.dma_start(
+                        out=out_0.rearrange("(g p j) w -> p g (j w)", p=P, j=PACK),
+                        in_=result_0[:].rearrange("p g j w -> p g (j w)"),
+                    )
+            elif kind == "c" and g == PASSES - 1:
+                evacuate_chunk(q)
 
-        def evacuate(count, share_with_vector):
-            batch, rest = pending[:count], pending[count:]
-            pending.clear()
-            pending.extend(rest)
-            for n, (bank, result, m, dst) in enumerate(batch):
-                if share_with_vector and n % 2 == 1:
-                    nc.vector.tensor_copy(out=result[:, m, :], in_=bank[:])
-                else:
-                    nc.scalar.copy(out=result[:, m, :], in_=bank[:])
-                if m == BLOCKS - 1:
-                    nc.sync.dma_start(out=dst, in_=result[:])
+        units = [("gt", 0, 0), ("w", 0, 0), ("gf", 0, 0)]
+        for g in range(1, PASSES):
+            units.extend([("gt", 0, g), ("gf", 0, g)])
+        units.extend([("c", 0, g) for g in range(PASSES)])
+        for g in range(PASSES - 1):
+            units.extend([("c", q, g) for q in range(1, CHUNKS)])
 
-        first_c = 1 + 2 * PASSES
         for step in range(-1, len(units) + 1):
             if step + 1 < len(units):
                 prepare(units[step + 1])
             if 0 <= step < len(units):
                 quantize_unit(units[step])
-            evacuate(BLOCKS if step <= first_c else 1, False)
+            if 0 <= step - 2:
+                evacuate_unit(units[step - 2])
             if 0 <= step - 1:
                 multiply_unit(units[step - 1])
-        evacuate(len(pending), True)
+
+        last = PASSES - 1
+        prepare(("c", 1, last))
+        prepare(("c", 2, last))
+        quantize_unit(("c", 1, last))
+        multiply_chunk(1, [last])
+        prepare(("c", 3, last))
+        quantize_unit(("c", 2, last))
+        multiply_chunk(2, [last])
+        quantize_unit(("c", 3, last))
+        evacuate_chunk(1)
+        store_halves(0, 4)
+        multiply_chunk(3, range(PASSES))
+        evacuate_chunk(2)
+        store_halves(4, 2)
+        evacuate_chunk(3)
+        store_halves(6, 1)
+        store_halves(7, 1)

from contextlib import ExitStack

import concourse.mybir as mybir
from concourse.masks import make_identity

TOKENS, UNITS, KAN_COLS = 2048, 512, 1536
FLOPS = 2 * TOKENS * UNITS * UNITS + 2 * TOKENS * (UNITS + KAN_COLS) * UNITS
BYTES = TOKENS * KAN_COLS * 4 + 2 * TOKENS * UNITS * 2 + UNITS * UNITS * 2 + 2 * TOKENS * UNITS * 4

F32 = mybir.dt.float32
BF16 = mybir.dt.bfloat16
U32 = mybir.dt.uint32
U8 = mybir.dt.uint8
E4M3 = mybir.dt.float8_e4m3fn_x4
E5M2 = mybir.dt.float8_e5m2_x4

P = 128
PACK = 4
K_PASS = P * PACK
PASSES = TOKENS // K_PASS
WIDTH = 512
BLOCKS = WIDTH // P
CHUNKS = (UNITS + KAN_COLS) // WIDTH
SCALAR_COLS = 224
RUN = 4


def tile_tkancell_pa_v_kernel(
    tc, x, lstm_out, kan_base_w, kan_spline_w, combine_w, combine_b, kan_concat, grad_out, out_0, out_1
):
    nc = tc.nc
    with ExitStack() as ctx:
        keep = ctx.enter_context(tc.tile_pool(name="keep", bufs=1))
        wide = ctx.enter_context(tc.tile_pool(name="wide", bufs=2))
        stage = ctx.enter_context(tc.tile_pool(name="stage", bufs=4))
        psum = ctx.enter_context(tc.psum_pool(name="psum", bufs=8))
        ctx.enter_context(tc.manual_schedule())

        def load_one(name, src, g):
            rows = keep.tile([P, PACK, src.shape[1]], src.dtype, name="%s%d" % (name, g), align_bytes=64)
            nc.sync.dma_start(
                out=rows[:], in_=src[g * K_PASS : (g + 1) * K_PASS, :].rearrange("(p j) w -> p j w", j=PACK)
            )
            return rows[:]

        def load_many(pool, name, src, first, count):
            many = pool.tile([P, count, PACK * WIDTH], BF16, name=name, tag=name, align_bytes=64)
            rows = src[first * K_PASS : (first + count) * K_PASS, :]
            nc.sync.dma_start(out=many[:], in_=rows.rearrange("(g p j) w -> p g (j w)", g=count, j=PACK))
            return [many[:, n, :].rearrange("p (j w) -> p j w", j=PACK) for n in range(count)]

        grad_rows = [load_one("grad", grad_out, 0)]
        w_rows = load_one("w", combine_w, 0)
        grad_rows = grad_rows + load_many(keep, "grad_rest", grad_out, 1, PASSES - 1)
        lstm_rows = load_many(wide, "wide", lstm_out, 0, PASSES)
        kan_rows = [load_one("kan", kan_concat, g) for g in range(PASSES)]

        def combined_rows(q, g):
            return lstm_rows[g] if q == 0 else kan_rows[g][:, :, (q - 1) * WIDTH : q * WIDTH]

        identity = keep.tile([P, P], F32, name="identity")
        make_identity(nc, identity[:])

        def new_grouped():
            return stage.tile([P, WIDTH, PACK], BF16, name="grouped", align_bytes=64)

        def new_bank():
            return psum.tile([P, WIDTH], F32, name="bank")

        def transpose_rows(rows, order):
            grouped = new_grouped()
            words = rows.bitcast(F32)
            grouped_words = grouped[:].rearrange("p c t -> p (c t)").bitcast(F32)
            banks = []
            for h in range(2):
                bank = new_bank()
                for jj in range(2):
                    for u in range(2):
                        col = (2 * jj + u) * P
                        nc.tensor.transpose(bank[:, col : col + P], words[:, 2 * h + jj, u : WIDTH // 2 : 2], identity[:])
                banks.append(bank)
            for h in range(2):
                dst = grouped_words.rearrange("p (%s u) -> p j r u" % order, j=PACK, u=2)[:, 2 * h : 2 * h + 2]
                src = banks[h][:].rearrange("p (j u r) -> p j r u", j=2, u=2)
                if order == "r j":
                    dst = dst.rearrange("p j r u -> p r j u")
                    src = src.rearrange("p j r u -> p r j u")
                nc.scalar.copy(out=dst, in_=src)
            return grouped

        def interleave_grad(rows):
            grouped = new_grouped()
            nc.vector.tensor_copy(
                out=grouped[:].rearrange("p (c i) t -> p c t i", i=RUN),
                in_=rows.rearrange("p t (c i) -> p c t i", i=RUN),
            )
            return grouped

        def interleave_combined(rows):
            grouped = new_grouped()
            dst = grouped[:].rearrange("p (e c i) t -> p c t i e", e=2, i=RUN // 2)
            src = rows.rearrange("p t (c i e) -> p c t i e", e=2, i=RUN // 2)
            cut = SCALAR_COLS // RUN
            nc.scalar.copy(out=dst[:, :cut], in_=src[:, :cut])
            nc.vector.tensor_copy(out=dst[:, cut:], in_=src[:, cut:])
            return grouped

        def quantize(grouped, fmt, pool, name):
            codes = pool.tile([P, WIDTH], U32, name=name + "_codes", align_bytes=64)
            scales = pool.tile([P, WIDTH], U8, name=name + "_scales", align_bytes=64)
            nc.vector.quantize_mx(
                out=codes[:].bitcast(fmt), scales=scales[:], in_=grouped[:].rearrange("p c t -> p (c t)")
            )
            return codes, scales, fmt

        def multiply(bank, m, stationary, moving, start, stop):
            cols = slice(m * P, (m + 1) * P)
            nc.tensor.matmul_mx(
                out=bank[:],
                lhsT=stationary[0][:, cols].bitcast(stationary[2]),
                lhsT_scale=stationary[1][:, cols],
                rhs=moving[0][:].bitcast(moving[2]),
                rhs_scale=moving[1][:],
                start=start,
                stop=stop,
            )

        grouped_of = {}
        quantized = {}
        banks_of = {}

        def prepare(unit):
            kind, q, g = unit
            if kind == "w":
                grouped_of[unit] = transpose_rows(w_rows, "r j")
            elif kind == "gf":
                grouped_of[unit] = transpose_rows(grad_rows[g], "j r")
            elif kind == "gt":
                grouped_of[unit] = interleave_grad(grad_rows[g])
            else:
                grouped_of[unit] = interleave_combined(combined_rows(q, g))

        def quantize_unit(unit):
            kind, q, g = unit
            if kind == "w":
                quantized[unit] = quantize(grouped_of[unit], E4M3, keep, "w")
            elif kind == "gf":
                quantized[unit] = quantize(grouped_of[unit], E5M2, stage, "lhs")
            elif kind == "gt":
                quantized[unit] = quantize(grouped_of[unit], E5M2, keep, "grad_tok%d" % g)
            elif q == CHUNKS - 1:
                quantized[unit] = quantize(grouped_of[unit], E4M3, keep, "late%d" % g)
            else:
                quantized[unit] = quantize(grouped_of[unit], E4M3, stage, "lhs")

        def evacuate(banks, result, vector_blocks):
            for n in range(BLOCKS):
                if n in vector_blocks:
                    nc.vector.tensor_copy(out=result[:, n, :], in_=banks[n][:])
                else:
                    nc.scalar.copy(out=result[:, n, :], in_=banks[n][:])

        def multiply_chunk(q, passes):
            if passes[0] == 0:
                banks_of[q] = [new_bank() for m in range(BLOCKS)]
            for n in range(BLOCKS):
                for g in passes:
                    stationary, moving = quantized[("c", q, g)], quantized[("gt", 0, g)]
                    block = 2 * (n % 2) + n // 2
                    multiply(banks_of[q][n], block, stationary, moving, g == 0, g == PASSES - 1)

        result_0 = keep.tile([P, PASSES, BLOCKS, WIDTH], F32, name="result_0")
        results_1 = {}

        def evacuate_chunk(q):
            if q % 2 == 0:
                results_1[q // 2] = wide.tile([P, 2, BLOCKS, WIDTH], F32, name="result_1", tag="wide", align_bytes=64)
            evacuate(banks_of[q], results_1[q // 2][:, q % 2], (1, 3))

        def store_halves(first, count):
            src = results_1[first // 4][:].rearrange("p q (h e) w -> p (q h) (e w)", e=2)
            rows = out_1[first * 2 * P : (first + count) * 2 * P, :]
            nc.sync.dma_start(
                out=rows.rearrange("(h p e) w -> p h (e w)", p=P, e=2),
                in_=src[:, first % 4 : first % 4 + count, :],
            )

        def multiply_unit(unit):
            kind, q, g = unit
            if kind == "gf":
                banks_of[unit] = [new_bank() for m in range(BLOCKS)]
                for m in range(BLOCKS):
                    multiply(banks_of[unit][m], m, quantized[unit], quantized[("w", 0, 0)], True, True)
            elif kind == "c" and q < CHUNKS - 1:
                multiply_chunk(q, [g])

        def evacuate_unit(unit):
            kind, q, g = unit
            if kind == "gf":
                evacuate(banks_of[unit], result_0[:, g], (3,))
                if g == PASSES - 1:
                    nc.sync.dma_start(
                        out=out_0.rearrange("(g p j) w -> p g (j w)", p=P, j=PACK),
                        in_=result_0[:].rearrange("p g j w -> p g (j w)"),
                    )
            elif kind == "c" and g == PASSES - 1:
                evacuate_chunk(q)

        units = [("gt", 0, 0), ("w", 0, 0), ("gf", 0, 0)]
        for g in range(1, PASSES):
            units.extend([("gt", 0, g), ("gf", 0, g)])
        units.extend([("c", 0, g) for g in range(PASSES)])
        for g in range(PASSES - 1):
            units.extend([("c", q, g) for q in range(1, CHUNKS)])

        for step in range(-1, len(units) + 1):
            if step + 1 < len(units):
                prepare(units[step + 1])
            if 0 <= step < len(units):
                quantize_unit(units[step])
            if 0 <= step - 2:
                evacuate_unit(units[step - 2])
            if 0 <= step - 1:
                multiply_unit(units[step - 1])

        last = PASSES - 1
        prepare(("c", 1, last))
        prepare(("c", 2, last))
        quantize_unit(("c", 1, last))
        multiply_chunk(1, [last])
        prepare(("c", 3, last))
        quantize_unit(("c", 2, last))
        multiply_chunk(2, [last])
        quantize_unit(("c", 3, last))
        evacuate_chunk(1)
        store_halves(0, 4)
        multiply_chunk(3, range(PASSES))
        evacuate_chunk(2)
        store_halves(4, 2)
        evacuate_chunk(3)
        store_halves(6, 1)
        store_halves(7, 1)
